import numpy as np
import ml_dtypes


def mxq(x, axis, fmt="e4m3"):
    dtype, down = {"e4m3": (ml_dtypes.float8_e4m3fn, 7), "e5m2": (ml_dtypes.float8_e5m2, 14)}[fmt]
    v = np.moveaxis(np.asarray(x, np.float32).astype(ml_dtypes.bfloat16).astype(np.float64), axis, -1)
    blocks = v.reshape(v.shape[:-1] + (-1, 32))
    amax = np.abs(blocks).max(-1, keepdims=True)
    byte = np.maximum(np.where(amax > 0, np.frexp(amax)[1] - 1 + 127, 0) - down, 1)
    scale = np.exp2(byte - 127.0)
    codes = (blocks / scale).astype(np.float32).astype(dtype).astype(np.float64)
    return np.moveaxis((codes * scale).reshape(v.shape), -1, axis)


WIDE = False


def mx_kscale(k):
    if not WIDE:
        return np.ones(k)
    levels = np.array([10, -10, 5, -5, 0])
    if k % 512:
        return np.exp2(np.random.permutation(np.resize(levels, k // 32))).repeat(32)
    a = np.empty((k // 512, 16))
    for p in range(k // 512):
        a[p, :8] = np.random.permutation(np.resize(levels, 8))
        for g in range(8):
            far = levels[np.abs(levels - a[p, g]) >= 10]
            a[p, g + 8] = far[np.random.randint(len(far))]
    return np.exp2(a.ravel()).repeat(32)


BF16 = ml_dtypes.bfloat16


def bf(x):
    return np.asarray(x, np.float32).astype(BF16)


def f64(x):
    return np.asarray(x).astype(np.float64)


B, N, HID, H, D = 2, 128, 2048, 16, 128


def apply_rope(t, rope):
    freqs = rope[:, 0, :]
    cos = np.repeat(freqs[:, 0::2], 2, axis=-1)[None, None]
    sin = np.repeat(freqs[:, 1::2], 2, axis=-1)[None, None]
    tr = t.reshape(*t.shape[:-1], -1, 2)
    t_real, t_imag = tr[..., 0], tr[..., 1]
    t_rot = np.stack([-t_imag, t_real], axis=-1).reshape(t.shape)
    return t * cos + t_rot * sin


def draw0():
    s = mx_kscale(HID)
    return {"x": bf(np.random.standard_normal((B, N, HID)) * s),
            "rope": bf(np.random.uniform(size=(N, 1, D))),
            "qkv_w": bf(np.random.standard_normal((HID, 3 * H * D)) * 1.5 / np.sqrt(HID) / s[:, None])}


def core(x, rope, qkv_w):
    r = f64(rope)
    qkv = (mxq(f64(x), 2, "e4m3") @ mxq(f64(qkv_w), 0, "e4m3")).reshape(B, N, 3, H, D)
    q = np.transpose(qkv[:, :, 0], (0, 2, 1, 3))
    k = np.transpose(qkv[:, :, 1], (0, 2, 1, 3))
    v = np.transpose(qkv[:, :, 2], (0, 2, 1, 3))
    return apply_rope(q, r), apply_rope(k, r), v


def e4m3fn_bytes(y):
    return np.clip(np.asarray(y, np.float64), -448.0, 448.0).astype(np.float32).astype(ml_dtypes.float8_e4m3fn).view(np.uint8)


def e4m3fn_values(b):
    return np.asarray(b, np.uint8).view(ml_dtypes.float8_e4m3fn).astype(np.float64)


def setup_inputs():
    d = draw0()
    x0 = np.asarray(d['qkv_w']).astype(np.float64)
    s = (np.max(np.abs(x0), axis=(1,), keepdims=True) / 448.0).astype(np.float32)
    out = {}
    for k, v in d.items():
        if k == 'qkv_w':
            out['qkv_w_bytes'] = e4m3fn_bytes(x0 / s.astype(np.float64))
            out['qkv_w_scale'] = s
        else:
            out[k] = v
    return out


def reference(x, rope, qkv_w_bytes, qkv_w_scale):
    return core(x, rope, e4m3fn_values(qkv_w_bytes) * qkv_w_scale.astype(np.float64))

@@ -1,0 +1,226 @@
+from contextlib import ExitStack
+
+import concourse.mybir as mybir
+from concourse.masks import make_identity
+
+F32 = mybir.dt.float32
+BF16 = mybir.dt.bfloat16
+U32 = mybir.dt.uint32
+U8 = mybir.dt.uint8
+FP8 = mybir.dt.float8_e4m3fn
+FP8X4 = mybir.dt.float8_e4m3fn_x4
+ACT = mybir.ActivationFunctionType
+ALU = mybir.AluOpType
+
+B, N, HID, H, D = 2, 128, 2048, 16, 128
+FLOPS = 2 * B * N * HID * 3 * H * D
+
+P = 128
+PACK = 4
+PASSES = HID // (P * PACK)
+CW = 1024
+NT = 512
+CHUNKS = ((0, 0), (1, 0), (2, 0), (0, 1), (1, 1), (2, 1))
+UNITS = len(CHUNKS) * PASSES
+V_WIDEN = ((0, 2), (0, 3))
+
+
+def tile_attention_pa_kernel(tc, x, rope, qkv_w_bytes, qkv_w_scale, out_0, out_1, out_2):
+    nc = tc.nc
+    outs = (out_0, out_1, out_2)
+    wb_view = qkv_w_bytes.rearrange("(g p t) n -> g p t n", p=P, t=PACK)
+
+    with ExitStack() as ctx:
+        const = ctx.enter_context(tc.tile_pool(name="const", bufs=1))
+        wpool = ctx.enter_context(tc.tile_pool(name="wpool", bufs=1))
+        widep = ctx.enter_context(tc.tile_pool(name="widep", bufs=3))
+        grpp = ctx.enter_context(tc.tile_pool(name="grpp", bufs=2))
+        codep = ctx.enter_context(tc.tile_pool(name="codep", bufs=3))
+        ropep = ctx.enter_context(tc.tile_pool(name="ropep", bufs=2))
+        outp = ctx.enter_context(tc.tile_pool(name="outp", bufs=3))
+        psum = ctx.enter_context(tc.psum_pool(name="psum", bufs=8))
+
+        ident = const.tile([P, P], F32)
+        make_identity(nc, ident[:])
+
+        ctx.enter_context(tc.manual_schedule())
+
+        wscale = const.tile([P, PASSES * PACK], F32)
+        nc.sync.dma_start(
+            out=wscale[:].rearrange("p (g t) -> p g t", t=PACK),
+            in_=qkv_w_scale.rearrange("(g p t) o -> p g (t o)", p=P, t=PACK),
+        )
+        wbytes = {}
+
+        def load_unit(u):
+            comp, half = CHUNKS[u // PASSES]
+            g = u % PASSES
+            c0 = comp * H * D + half * CW
+            wb = wpool.tile([P, PACK, CW], U8, name="wbytes%d" % u)
+            nc.sync.dma_start(out=wb[:], in_=wb_view[g, :, :, c0 : c0 + CW])
+            wbytes[u] = wb
+
+        load_unit(0)
+        x_sb = const.tile([P, B, HID], BF16)
+        for b in range(B):
+            nc.sync.dma_start(out=x_sb[:, b, :], in_=x[b])
+        rope_sb = const.tile([P, D], BF16)
+        nc.sync.dma_start(out=rope_sb[:], in_=rope.rearrange("n o d -> n (o d)"))
+        for u in range(1, UNITS):
+            load_unit(u)
+
+        warm = const.tile([P, 1], F32)
+        warm2 = const.tile([P, 1], F32)
+        nc.gpsimd.memset(warm[:], 0.0)
+        nc.scalar.activation(out=warm2[:], in_=warm[:], func=ACT.Copy)
+
+        cos4 = const.tile([P, NT], F32)
+        sin4 = const.tile([P, NT], F32)
+        rv = rope_sb[:].rearrange("p (j e) -> p j e", e=2)
+        cv = cos4[:, 0:D].rearrange("p (j e) -> p j e", e=2)
+        sv = sin4[:, 0:D].rearrange("p (j e) -> p j e", e=2)
+        nc.gpsimd.tensor_copy(out=cv[:, :, 0:1], in_=rv[:, :, 0:1])
+        nc.gpsimd.tensor_copy(out=cv[:, :, 1:2], in_=rv[:, :, 0:1])
+        nc.gpsimd.tensor_scalar(out=sv[:, :, 0:1], in0=rv[:, :, 1:2], scalar1=-1.0, scalar2=0.0, op0=ALU.mult, op1=ALU.add)
+        nc.gpsimd.tensor_copy(out=sv[:, :, 1:2], in_=rv[:, :, 1:2])
+        for tab in (cos4, sin4):
+            nc.gpsimd.tensor_copy(out=tab[:, D : 2 * D], in_=tab[:, 0:D])
+            nc.gpsimd.tensor_copy(out=tab[:, 2 * D : 4 * D], in_=tab[:, 0 : 2 * D])
+
+        wide_t, grp_t, code_t, scl_t, acc_t = {}, {}, {}, {}, {}
+
+        def widen(u):
+            g = u % PASSES
+            wide = widep.tile([P, PACK, CW], BF16)
+            wide_t[u] = wide
+            for t in range(PACK):
+                col = wscale[:, PACK * g + t : PACK * g + t + 1]
+                src = wbytes[u][:, t, :].bitcast(FP8)
+                if (u, t) in V_WIDEN:
+                    nc.vector.tensor_scalar(out=wide[:, t, :], in0=src, scalar1=col, scalar2=None, op0=ALU.mult)
+                else:
+                    nc.scalar.activation(out=wide[:, t, :], in_=src, func=ACT.Copy, scale=col)
+
+        def inter(u):
+            grp = grpp.tile([P, CW * PACK], BF16, align_bytes=64)
+            grp_t[u] = grp
+            nc.vector.tensor_copy(
+                out=grp[:].rearrange("p (n t) -> p n t", t=PACK),
+                in_=wide_t[u][:].rearrange("p t n -> p n t"),
+            )
+
+        def quant(u):
+            codes = codep.tile([P, CW], U32, align_bytes=64)
+            scl = codep.tile([P, CW], U8, align_bytes=64)
+            code_t[u] = codes
+            scl_t[u] = scl
+            nc.vector.quantize_mx(out=codes[:].bitcast(FP8X4), scales=scl[:], in_=grp_t[u][:])
+
+        x_grp = const.tile([P, PASSES * B * N * PACK], BF16, align_bytes=64)
+        x_codes = const.tile([P, PASSES * B * N], U32, align_bytes=64)
+        x_scl = const.tile([P, PASSES * B * N], U8, align_bytes=64)
+
+        def x_transposes():
+            xw = x_grp[:].bitcast(F32).rearrange("p (g b r u) -> p g b r u", g=PASSES, b=B, u=2)
+            for b in range(B):
+                words = x_sb[:, b, :].bitcast(F32)
+                for gp in range(PASSES // 2):
+                    xt = psum.tile([P, 4, N], F32, tag="bank")
+                    for gl in range(2):
+                        g = 2 * gp + gl
+                        for u in range(2):
+                            nc.tensor.transpose(xt[:, 2 * gl + u, :], words[:, 256 * g + u : 256 * (g + 1) : 2], ident[:])
+                    nc.vector.tensor_copy(
+                        out=xw[:, 2 * gp : 2 * gp + 2, b, :, :],
+                        in_=xt[:].rearrange("p (g u) r -> p g r u", u=2),
+                    )
+
+        def x_quant():
+            nc.vector.quantize_mx(out=x_codes[:].bitcast(FP8X4), scales=x_scl[:], in_=x_grp[:])
+
+        def mm(u):
+            c, g = u // PASSES, u % PASSES
+            for b in range(B):
+                for nh in range(CW // NT):
+                    if g == 0:
+                        acc = psum.tile([P, NT], F32, tag="bank")
+                        acc_t[(c, b, nh)] = acc
+                    xc = slice((g * B + b) * N, (g * B + b + 1) * N)
+                    wc = slice(nh * NT, (nh + 1) * NT)
+                    nc.tensor.matmul_mx(
+                        out=acc_t[(c, b, nh)][:],
+                        lhsT=x_codes[:, xc].bitcast(FP8X4),
+                        lhsT_scale=x_scl[:, xc],
+                        rhs=code_t[u][:, wc].bitcast(FP8X4),
+                        rhs_scale=scl_t[u][:, wc],
+                        start=(g == 0),
+                        stop=(g == PASSES - 1),
+                    )
+
+        def store(job, res):
+            c, b, nh = job
+            comp, half = CHUNKS[c]
+            h0 = (half * CW + nh * NT) // D
+            nc.sync.dma_start(
+                out=outs[comp][b, h0 : h0 + NT // D].rearrange("h n d -> n h d"),
+                in_=res[:].rearrange("p (h d) -> p h d", d=D),
+            )
+
+        def rope_mults(job):
+            acc = acc_t[job]
+            ra = ropep.tile([P, NT], F32)
+            rb = ropep.tile([P, NT], F32)
+            nc.vector.tensor_tensor(out=ra[:], in0=acc[:], in1=cos4[:], op=ALU.mult)
+            nc.vector.tensor_tensor(
+                out=rb[:].rearrange("p (j e) -> p j e", e=2),
+                in0=acc[:].rearrange("p (j e) -> p j e", e=2)[:, :, ::-1],
+                in1=sin4[:].rearrange("p (j e) -> p j e", e=2),
+                op=ALU.mult,
+            )
+            return ra, rb
+
+        def rope_add(job, ra, rb):
+            res = outp.tile([P, NT], F32)
+            nc.vector.tensor_tensor(out=res[:], in0=ra[:], in1=rb[:], op=ALU.add)
+            store(job, res)
+
+        def plain_out(job, engine):
+            res = outp.tile([P, NT], F32)
+            if engine == "s":
+                nc.scalar.copy(out=res[:], in_=acc_t[job][:])
+            else:
+                nc.vector.tensor_copy(out=res[:], in_=acc_t[job][:])
+            store(job, res)
+
+        jobs = []
+        done = 0
+        for s in range(UNITS + 3):
+            if s < UNITS:
+                widen(s)
+            if 1 <= s <= UNITS:
+                inter(s - 1)
+            if s == 1:
+                x_transposes()
+            job = None
+            if done < len(jobs):
+                job = jobs[done]
+                done += 1
+            parts = None
+            if job is not None:
+                if CHUNKS[job[0]][0] == 2:
+                    plain_out(job, "s")
+                else:
+                    parts = rope_mults(job)
+            if s == 2:
+                x_quant()
+            if 2 <= s <= UNITS + 1:
+                quant(s - 2)
+            if parts is not None:
+                rope_add(job, parts[0], parts[1])
+            if s >= 3:
+                mm(s - 3)
+                if (s - 3) % PASSES == PASSES - 1:
+                    c = (s - 3) // PASSES
+                    jobs.extend([(c, b, nh) for b in range(B) for nh in range(CW // NT)])
+        for i, job in enumerate(jobs[done:]):
+            plain_out(job, "s" if i % 2 == 0 else "v")

@@ -105,8 +105,8 @@ def tile_attention_pa_kernel(tc, x, rope, qkv_w_bytes, qkv_w_scale, out_0, out_1
             grp = grpp.tile([P, CW * PACK], BF16, align_bytes=64)
             grp_t[u] = grp
             nc.vector.tensor_copy(
-                out=grp[:].rearrange("p (n t) -> p n t", t=PACK),
-                in_=wide_t[u][:].rearrange("p t n -> p n t"),
+                out=grp[:].rearrange("p (c i t) -> p c t i", i=4, t=PACK),
+                in_=wide_t[u][:].rearrange("p t (c i) -> p c t i", i=4),
             )
 
         def quant(u):

@@ -18,11 +18,15 @@ FLOPS = 2 * B * N * HID * 3 * H * D
 P = 128
 PACK = 4
 PASSES = HID // (P * PACK)
-CW = 1024
 NT = 512
-CHUNKS = ((0, 0), (1, 0), (2, 0), (0, 1), (1, 1), (2, 1))
+CHUNKS = ((0, 0, 1024), (1, 0, 1024), (2, 0, 1024), (0, 1024, 1024), (1, 1024, 1024), (2, 1024, 512), (2, 1536, 512))
 UNITS = len(CHUNKS) * PASSES
-V_WIDEN = ((0, 2), (0, 3))
+V_PLANES = (3, 0, 2, 0, 0, 0, 0, 0, 0, 0, 0, 0, 0, 0, 0, 0, 0, 0, 1, 0, 0, 0, 1, 0, 0, 0, 0, 0)
+S_COLS = (0, 0, 0, 0, 0, 0, 0, 0, 0, 0, 0, 0, 0, 0, 0, 0, 0, 512, 512, 0, 0, 512, 128, 0, 0, 0, 256, 0)
+G_ADDS = 3
+BURST = True
+X_AFTER = 1
+RUN = 4
 
 
 def tile_attention_pa_kernel(tc, x, rope, qkv_w_bytes, qkv_w_scale, out_0, out_1, out_2):
@@ -33,11 +37,11 @@ def tile_attention_pa_kernel(tc, x, rope, qkv_w_bytes, qkv_w_scale, out_0, out_1
     with ExitStack() as ctx:
         const = ctx.enter_context(tc.tile_pool(name="const", bufs=1))
         wpool = ctx.enter_context(tc.tile_pool(name="wpool", bufs=1))
-        widep = ctx.enter_context(tc.tile_pool(name="widep", bufs=3))
+        widep = ctx.enter_context(tc.tile_pool(name="widep", bufs=4))
         grpp = ctx.enter_context(tc.tile_pool(name="grpp", bufs=2))
         codep = ctx.enter_context(tc.tile_pool(name="codep", bufs=3))
-        ropep = ctx.enter_context(tc.tile_pool(name="ropep", bufs=2))
-        outp = ctx.enter_context(tc.tile_pool(name="outp", bufs=3))
+        ropep = ctx.enter_context(tc.tile_pool(name="ropep", bufs=4))
+        outp = ctx.enter_context(tc.tile_pool(name="outp", bufs=4))
         psum = ctx.enter_context(tc.psum_pool(name="psum", bufs=8))
 
         ident = const.tile([P, P], F32)
@@ -46,28 +50,35 @@ def tile_attention_pa_kernel(tc, x, rope, qkv_w_bytes, qkv_w_scale, out_0, out_1
         ctx.enter_context(tc.manual_schedule())
 
         wscale = const.tile([P, PASSES * PACK], F32)
-        nc.sync.dma_start(
+        nc.scalar.dma_start(
             out=wscale[:].rearrange("p (g t) -> p g t", t=PACK),
             in_=qkv_w_scale.rearrange("(g p t) o -> p g (t o)", p=P, t=PACK),
         )
-        wbytes = {}
+        planes = {}
 
         def load_unit(u):
-            comp, half = CHUNKS[u // PASSES]
+            comp, col, w = CHUNKS[u // PASSES]
             g = u % PASSES
-            c0 = comp * H * D + half * CW
-            wb = wpool.tile([P, PACK, CW], U8, name="wbytes%d" % u)
-            nc.sync.dma_start(out=wb[:], in_=wb_view[g, :, :, c0 : c0 + CW])
-            wbytes[u] = wb
+            c0 = comp * H * D + col
+            if u == 0:
+                for t in range(PACK):
+                    wb1 = wpool.tile([P, w], U8, name="wbytes0_%d" % t)
+                    nc.sync.dma_start(out=wb1[:], in_=wb_view[g, :, t, c0 : c0 + w])
+                    planes[(u, t)] = wb1[:]
+            else:
+                wb = wpool.tile([P, PACK, w], U8, name="wbytes%d" % u)
+                nc.sync.dma_start(out=wb[:], in_=wb_view[g, :, :, c0 : c0 + w])
+                for t in range(PACK):
+                    planes[(u, t)] = wb[:, t, :]
 
-        load_unit(0)
         x_sb = const.tile([P, B, HID], BF16)
-        for b in range(B):
-            nc.sync.dma_start(out=x_sb[:, b, :], in_=x[b])
         rope_sb = const.tile([P, D], BF16)
-        nc.sync.dma_start(out=rope_sb[:], in_=rope.rearrange("n o d -> n (o d)"))
-        for u in range(1, UNITS):
+        for u in range(UNITS):
             load_unit(u)
+            if u == X_AFTER:
+                for b in range(B):
+                    nc.sync.dma_start(out=x_sb[:, b, :], in_=x[b])
+                nc.sync.dma_start(out=rope_sb[:], in_=rope.rearrange("n o d -> n (o d)"))
 
         warm = const.tile([P, 1], F32)
         warm2 = const.tile([P, 1], F32)
@@ -89,29 +100,41 @@ def tile_attention_pa_kernel(tc, x, rope, qkv_w_bytes, qkv_w_scale, out_0, out_1
 
         wide_t, grp_t, code_t, scl_t, acc_t = {}, {}, {}, {}, {}
 
+        def width(u):
+            return CHUNKS[u // PASSES][2]
+
         def widen(u):
             g = u % PASSES
-            wide = widep.tile([P, PACK, CW], BF16)
+            wide = widep.tile([P, PACK, width(u)], BF16)
             wide_t[u] = wide
             for t in range(PACK):
                 col = wscale[:, PACK * g + t : PACK * g + t + 1]
-                src = wbytes[u][:, t, :].bitcast(FP8)
-                if (u, t) in V_WIDEN:
+                src = planes[(u, t)].bitcast(FP8)
+                if t >= PACK - V_PLANES[u]:
                     nc.vector.tensor_scalar(out=wide[:, t, :], in0=src, scalar1=col, scalar2=None, op0=ALU.mult)
                 else:
                     nc.scalar.activation(out=wide[:, t, :], in_=src, func=ACT.Copy, scale=col)
 
         def inter(u):
-            grp = grpp.tile([P, CW * PACK], BF16, align_bytes=64)
+            w = width(u)
+            grp = grpp.tile([P, w * PACK], BF16, align_bytes=64)
             grp_t[u] = grp
-            nc.vector.tensor_copy(
-                out=grp[:].rearrange("p (c i t) -> p c t i", i=4, t=PACK),
-                in_=wide_t[u][:].rearrange("p t (c i) -> p c t i", i=4),
-            )
+            cut = w - S_COLS[u]
+            if cut > 0:
+                nc.vector.tensor_copy(
+                    out=grp[:, 0 : cut * PACK].rearrange("p (c i t) -> p c t i", i=RUN, t=PACK),
+                    in_=wide_t[u][:, :, 0:cut].rearrange("p t (c i) -> p c t i", i=RUN),
+                )
+            if cut < w:
+                nc.scalar.copy(
+                    out=grp[:, cut * PACK : w * PACK].rearrange("p (c i t) -> p c t i", i=RUN, t=PACK),
+                    in_=wide_t[u][:, :, cut:w].rearrange("p t (c i) -> p c t i", i=RUN),
+                )
 
         def quant(u):
-            codes = codep.tile([P, CW], U32, align_bytes=64)
-            scl = codep.tile([P, CW], U8, align_bytes=64)
+            w = width(u)
+            codes = codep.tile([P, w], U32, align_bytes=64)
+            scl = codep.tile([P, w], U8, align_bytes=64)
             code_t[u] = codes
             scl_t[u] = scl
             nc.vector.quantize_mx(out=codes[:].bitcast(FP8X4), scales=scl[:], in_=grp_t[u][:])
@@ -141,7 +164,7 @@ def tile_attention_pa_kernel(tc, x, rope, qkv_w_bytes, qkv_w_scale, out_0, out_1
         def mm(u):
             c, g = u // PASSES, u % PASSES
             for b in range(B):
-                for nh in range(CW // NT):
+                for nh in range(width(u) // NT):
                     if g == 0:
                         acc = psum.tile([P, NT], F32, tag="bank")
                         acc_t[(c, b, nh)] = acc
@@ -159,8 +182,8 @@ def tile_attention_pa_kernel(tc, x, rope, qkv_w_bytes, qkv_w_scale, out_0, out_1
 
         def store(job, res):
             c, b, nh = job
-            comp, half = CHUNKS[c]
-            h0 = (half * CW + nh * NT) // D
+            comp, col, w = CHUNKS[c]
+            h0 = (col + nh * NT) // D
             nc.sync.dma_start(
                 out=outs[comp][b, h0 : h0 + NT // D].rearrange("h n d -> n h d"),
                 in_=res[:].rearrange("p (h d) -> p h d", d=D),
@@ -179,14 +202,14 @@ def tile_attention_pa_kernel(tc, x, rope, qkv_w_bytes, qkv_w_scale, out_0, out_1
             )
             return ra, rb
 
-        def rope_add(job, ra, rb):
+        def rope_add(job, ra, rb, engine):
             res = outp.tile([P, NT], F32)
-            nc.vector.tensor_tensor(out=res[:], in0=ra[:], in1=rb[:], op=ALU.add)
+            engine.tensor_tensor(out=res[:], in0=ra[:], in1=rb[:], op=ALU.add)
             store(job, res)
 
-        def plain_out(job, engine):
+        def plain_out(job, on_scalar):
             res = outp.tile([P, NT], F32)
-            if engine == "s":
+            if on_scalar:
                 nc.scalar.copy(out=res[:], in_=acc_t[job][:])
             else:
                 nc.vector.tensor_copy(out=res[:], in_=acc_t[job][:])
@@ -201,26 +224,31 @@ def tile_attention_pa_kernel(tc, x, rope, qkv_w_bytes, qkv_w_scale, out_0, out_1
                 inter(s - 1)
             if s == 1:
                 x_transposes()
-            job = None
-            if done < len(jobs):
+            late = []
+            take = len(jobs) - done
+            if not BURST:
+                take = min(1, take)
+            for i in range(take):
                 job = jobs[done]
                 done += 1
-            parts = None
-            if job is not None:
                 if CHUNKS[job[0]][0] == 2:
-                    plain_out(job, "s")
+                    plain_out(job, True)
                 else:
-                    parts = rope_mults(job)
+                    ra, rb = rope_mults(job)
+                    if BURST and i < G_ADDS:
+                        rope_add(job, ra, rb, nc.gpsimd)
+                    else:
+                        late.append((job, ra, rb))
             if s == 2:
                 x_quant()
             if 2 <= s <= UNITS + 1:
                 quant(s - 2)
-            if parts is not None:
-                rope_add(job, parts[0], parts[1])
+            for job, ra, rb in late:
+                rope_add(job, ra, rb, nc.vector)
             if s >= 3:
                 mm(s - 3)
                 if (s - 3) % PASSES == PASSES - 1:
                     c = (s - 3) // PASSES
-                    jobs.extend([(c, b, nh) for b in range(B) for nh in range(CW // NT)])
+                    jobs.extend([(c, b, nh) for b in range(B) for nh in range(CHUNKS[c][2] // NT)])
         for i, job in enumerate(jobs[done:]):
-            plain_out(job, "s" if i % 2 == 0 else "v")
+            plain_out(job, i % 2 == 0)

@@ -26,7 +26,7 @@ S_COLS = (0, 0, 0, 0, 0, 0, 0, 0, 0, 0, 0, 0, 0, 0, 0, 0, 0, 512, 512, 0, 0, 512
 G_ADDS = 3
 BURST = True
 X_AFTER = 1
-RUN = 4
+RUN = 8
 
 
 def tile_attention_pa_kernel(tc, x, rope, qkv_w_bytes, qkv_w_scale, out_0, out_1, out_2):

@@ -23,7 +23,8 @@ CHUNKS = ((0, 0, 1024), (1, 0, 1024), (2, 0, 1024), (0, 1024, 1024), (1, 1024, 1
 UNITS = len(CHUNKS) * PASSES
 V_PLANES = (3, 0, 2, 0, 0, 0, 0, 0, 0, 0, 0, 0, 0, 0, 0, 0, 0, 0, 1, 0, 0, 0, 1, 0, 0, 0, 0, 0)
 S_COLS = (0, 0, 0, 0, 0, 0, 0, 0, 0, 0, 0, 0, 0, 0, 0, 0, 0, 512, 512, 0, 0, 512, 128, 0, 0, 0, 256, 0)
-G_ADDS = 3
+G_ADDS = 4
+PE_MAX = 768
 BURST = True
 X_AFTER = 1
 RUN = 8
@@ -46,6 +47,8 @@ def tile_attention_pa_kernel(tc, x, rope, qkv_w_bytes, qkv_w_scale, out_0, out_1
 
         ident = const.tile([P, P], F32)
         make_identity(nc, ident[:])
+        identb = const.tile([P, P], BF16)
+        make_identity(nc, identb[:])
 
         ctx.enter_context(tc.manual_schedule())
 
@@ -98,7 +101,13 @@ def tile_attention_pa_kernel(tc, x, rope, qkv_w_bytes, qkv_w_scale, out_0, out_1
             nc.gpsimd.tensor_copy(out=tab[:, D : 2 * D], in_=tab[:, 0:D])
             nc.gpsimd.tensor_copy(out=tab[:, 2 * D : 4 * D], in_=tab[:, 0 : 2 * D])
 
-        wide_t, grp_t, code_t, scl_t, acc_t = {}, {}, {}, {}, {}
+        wide_t, grp_t, code_t, scl_t, acc_t, il_t = {}, {}, {}, {}, {}, {}
+
+        def pe_cols(u):
+            c = u - PASSES - 2
+            if c >= 0 and c % PASSES == 0 and CHUNKS[c // PASSES][0] != 2:
+                return min(PE_MAX, width(u) - S_COLS[u])
+            return 0
 
         def width(u):
             return CHUNKS[u // PASSES][2]
@@ -120,16 +129,34 @@ def tile_attention_pa_kernel(tc, x, rope, qkv_w_bytes, qkv_w_scale, out_0, out_1
             grp = grpp.tile([P, w * PACK], BF16, align_bytes=64)
             grp_t[u] = grp
             cut = w - S_COLS[u]
-            if cut > 0:
+            cv = cut - pe_cols(u)
+            if cv > 0:
                 nc.vector.tensor_copy(
-                    out=grp[:, 0 : cut * PACK].rearrange("p (c i t) -> p c t i", i=RUN, t=PACK),
-                    in_=wide_t[u][:, :, 0:cut].rearrange("p t (c i) -> p c t i", i=RUN),
+                    out=grp[:, 0 : cv * PACK].rearrange("p (c i t) -> p c t i", i=RUN, t=PACK),
+                    in_=wide_t[u][:, :, 0:cv].rearrange("p t (c i) -> p c t i", i=RUN),
                 )
+            il_t[u] = []
+            for c0 in range(cv, cut, 2 * P):
+                n = min(2 * P, cut - c0)
+                il = psum.tile([P, 2 * P * PACK], BF16, tag="bank")
+                il_t[u].append((c0, n, il))
+                for h in range(0, n, P):
+                    nc.tensor.matmul(
+                        out=il[:, h * PACK : (h + P) * PACK],
+                        lhsT=identb[:],
+                        rhs=wide_t[u][:, :, c0 + h : c0 + h + P].rearrange("p t c -> p c t"),
+                        start=True,
+                        stop=True,
+                    )
             if cut < w:
                 nc.scalar.copy(
                     out=grp[:, cut * PACK : w * PACK].rearrange("p (c i t) -> p c t i", i=RUN, t=PACK),
                     in_=wide_t[u][:, :, cut:w].rearrange("p t (c i) -> p c t i", i=RUN),
                 )
+
+        def evac(u):
+            for c0, n, il in il_t[u]:
+                nc.vector.tensor_copy(out=grp_t[u][:, c0 * PACK : (c0 + n) * PACK], in_=il[:, 0 : n * PACK])
 
         def quant(u):
             w = width(u)
@@ -239,6 +266,8 @@ def tile_attention_pa_kernel(tc, x, rope, qkv_w_bytes, qkv_w_scale, out_0, out_1
                         rope_add(job, ra, rb, nc.gpsimd)
                     else:
                         late.append((job, ra, rb))
+            if 1 <= s <= UNITS:
+                evac(s - 1)
             if s == 2:
                 x_quant()
             if 2 <= s <= UNITS + 1:

@@ -88,18 +88,17 @@ def tile_attention_pa_kernel(tc, x, rope, qkv_w_bytes, qkv_w_scale, out_0, out_1
         nc.gpsimd.memset(warm[:], 0.0)
         nc.scalar.activation(out=warm2[:], in_=warm[:], func=ACT.Copy)
 
-        cos4 = const.tile([P, NT], F32)
-        sin4 = const.tile([P, NT], F32)
+        tab = const.tile([P, 2, NT], F32)
         rv = rope_sb[:].rearrange("p (j e) -> p j e", e=2)
-        cv = cos4[:, 0:D].rearrange("p (j e) -> p j e", e=2)
-        sv = sin4[:, 0:D].rearrange("p (j e) -> p j e", e=2)
+        cv = tab[:, 0, 0:D].rearrange("p (j e) -> p j e", e=2)
+        sv = tab[:, 1, 0:D].rearrange("p (j e) -> p j e", e=2)
         nc.gpsimd.tensor_copy(out=cv[:, :, 0:1], in_=rv[:, :, 0:1])
         nc.gpsimd.tensor_copy(out=cv[:, :, 1:2], in_=rv[:, :, 0:1])
-        nc.gpsimd.tensor_scalar(out=sv[:, :, 0:1], in0=rv[:, :, 1:2], scalar1=-1.0, scalar2=0.0, op0=ALU.mult, op1=ALU.add)
-        nc.gpsimd.tensor_copy(out=sv[:, :, 1:2], in_=rv[:, :, 1:2])
-        for tab in (cos4, sin4):
-            nc.gpsimd.tensor_copy(out=tab[:, D : 2 * D], in_=tab[:, 0:D])
-            nc.gpsimd.tensor_copy(out=tab[:, 2 * D : 4 * D], in_=tab[:, 0 : 2 * D])
+        nc.gpsimd.tensor_copy(out=sv[:, :, 0:1], in_=rv[:, :, 1:2])
+        nc.gpsimd.tensor_scalar(out=sv[:, :, 1:2], in0=rv[:, :, 1:2], scalar1=-1.0, scalar2=0.0, op0=ALU.mult, op1=ALU.add)
+        for r in range(2):
+            nc.gpsimd.tensor_copy(out=tab[:, r, D : 2 * D], in_=tab[:, r, 0:D])
+            nc.gpsimd.tensor_copy(out=tab[:, r, 2 * D : 4 * D], in_=tab[:, r, 0 : 2 * D])
 
         wide_t, grp_t, code_t, scl_t, acc_t, il_t = {}, {}, {}, {}, {}, {}
 
@@ -218,20 +217,23 @@ def tile_attention_pa_kernel(tc, x, rope, qkv_w_bytes, qkv_w_scale, out_0, out_1
 
         def rope_mults(job):
             acc = acc_t[job]
-            ra = ropep.tile([P, NT], F32)
-            rb = ropep.tile([P, NT], F32)
-            nc.vector.tensor_tensor(out=ra[:], in0=acc[:], in1=cos4[:], op=ALU.mult)
+            rr = ropep.tile([P, 2, NT], F32)
             nc.vector.tensor_tensor(
-                out=rb[:].rearrange("p (j e) -> p j e", e=2),
-                in0=acc[:].rearrange("p (j e) -> p j e", e=2)[:, :, ::-1],
-                in1=sin4[:].rearrange("p (j e) -> p j e", e=2),
+                out=rr[:],
+                in0=acc[:].rearrange("p (o n) -> p o n", o=1).to_broadcast([P, 2, NT]),
+                in1=tab[:],
                 op=ALU.mult,
             )
-            return ra, rb
+            return rr[:, 0, :], rr[:, 1, :]
 
         def rope_add(job, ra, rb, engine):
             res = outp.tile([P, NT], F32)
-            engine.tensor_tensor(out=res[:], in0=ra[:], in1=rb[:], op=ALU.add)
+            engine.tensor_tensor(
+                out=res[:].rearrange("p (j e) -> p j e", e=2),
+                in0=ra.rearrange("p (j e) -> p j e", e=2),
+                in1=rb.rearrange("p (j e) -> p j e", e=2)[:, :, ::-1],
+                op=ALU.add,
+            )
             store(job, res)
 
         def plain_out(job, on_scalar):

@@ -28,6 +28,7 @@ PE_MAX = 768
 BURST = True
 X_AFTER = 1
 RUN = 8
+TABLE_STEP = 4
 
 
 def tile_attention_pa_kernel(tc, x, rope, qkv_w_bytes, qkv_w_scale, out_0, out_1, out_2):
@@ -88,17 +89,16 @@ def tile_attention_pa_kernel(tc, x, rope, qkv_w_bytes, qkv_w_scale, out_0, out_1
         nc.gpsimd.memset(warm[:], 0.0)
         nc.scalar.activation(out=warm2[:], in_=warm[:], func=ACT.Copy)
 
-        tab = const.tile([P, 2, NT], F32)
-        rv = rope_sb[:].rearrange("p (j e) -> p j e", e=2)
-        cv = tab[:, 0, 0:D].rearrange("p (j e) -> p j e", e=2)
-        sv = tab[:, 1, 0:D].rearrange("p (j e) -> p j e", e=2)
-        nc.gpsimd.tensor_copy(out=cv[:, :, 0:1], in_=rv[:, :, 0:1])
-        nc.gpsimd.tensor_copy(out=cv[:, :, 1:2], in_=rv[:, :, 0:1])
-        nc.gpsimd.tensor_copy(out=sv[:, :, 0:1], in_=rv[:, :, 1:2])
-        nc.gpsimd.tensor_scalar(out=sv[:, :, 1:2], in0=rv[:, :, 1:2], scalar1=-1.0, scalar2=0.0, op0=ALU.mult, op1=ALU.add)
-        for r in range(2):
-            nc.gpsimd.tensor_copy(out=tab[:, r, D : 2 * D], in_=tab[:, r, 0:D])
-            nc.gpsimd.tensor_copy(out=tab[:, r, 2 * D : 4 * D], in_=tab[:, r, 0 : 2 * D])
+        tab = const.tile([P, 2, D], F32)
+
+        def rope_table():
+            rv = rope_sb[:].rearrange("p (j e) -> p j e", e=2)
+            sv = tab[:, 1, :].rearrange("p (j e) -> p j e", e=2)
+            nc.vector.tensor_copy(
+                out=tab[:, 0, :].rearrange("p (j e) -> p j e", e=2), in_=rv[:, :, 0:1].to_broadcast([P, D // 2, 2])
+            )
+            nc.vector.tensor_copy(out=sv[:, :, 0:1], in_=rv[:, :, 1:2])
+            nc.vector.tensor_scalar(out=sv[:, :, 1:2], in0=rv[:, :, 1:2], scalar1=-1.0, scalar2=None, op0=ALU.mult)
 
         wide_t, grp_t, code_t, scl_t, acc_t, il_t = {}, {}, {}, {}, {}, {}
 
@@ -219,9 +219,9 @@ def tile_attention_pa_kernel(tc, x, rope, qkv_w_bytes, qkv_w_scale, out_0, out_1
             acc = acc_t[job]
             rr = ropep.tile([P, 2, NT], F32)
             nc.vector.tensor_tensor(
-                out=rr[:],
-                in0=acc[:].rearrange("p (o n) -> p o n", o=1).to_broadcast([P, 2, NT]),
-                in1=tab[:],
+                out=rr[:].rearrange("p r (h d) -> p r h d", d=D),
+                in0=acc[:].rearrange("p (o h d) -> p o h d", o=1, d=D).to_broadcast([P, 2, NT // D, D]),
+                in1=tab[:].rearrange("p r (o d) -> p r o d", o=1).to_broadcast([P, 2, NT // D, D]),
                 op=ALU.mult,
             )
             return rr[:, 0, :], rr[:, 1, :]
@@ -253,6 +253,8 @@ def tile_attention_pa_kernel(tc, x, rope, qkv_w_bytes, qkv_w_scale, out_0, out_1
                 inter(s - 1)
             if s == 1:
                 x_transposes()
+            if s == TABLE_STEP:
+                rope_table()
             late = []
             take = len(jobs) - done
             if not BURST:

@@ -22,9 +22,9 @@ NT = 512
 CHUNKS = ((0, 0, 1024), (1, 0, 1024), (2, 0, 1024), (0, 1024, 1024), (1, 1024, 1024), (2, 1024, 512), (2, 1536, 512))
 UNITS = len(CHUNKS) * PASSES
 V_PLANES = (3, 0, 2, 0, 0, 0, 0, 0, 0, 0, 0, 0, 0, 0, 0, 0, 0, 0, 1, 0, 0, 0, 1, 0, 0, 0, 0, 0)
-S_COLS = (0, 0, 0, 0, 0, 0, 0, 0, 0, 0, 0, 0, 0, 0, 0, 0, 0, 512, 512, 0, 0, 512, 128, 0, 0, 0, 256, 0)
+S_COLS = (0, 0, 0, 0, 0, 0, 0, 0, 0, 0, 0, 0, 0, 0, 0, 0, 0, 512, 256, 256, 0, 512, 0, 128, 0, 0, 256, 0)
 G_ADDS = 4
-PE_MAX = 768
+PE_MAX = 1024
 BURST = True
 X_AFTER = 1
 RUN = 8
@@ -155,7 +155,9 @@ def tile_attention_pa_kernel(tc, x, rope, qkv_w_bytes, qkv_w_scale, out_0, out_1
 
         def evac(u):
             for c0, n, il in il_t[u]:
-                nc.vector.tensor_copy(out=grp_t[u][:, c0 * PACK : (c0 + n) * PACK], in_=il[:, 0 : n * PACK])
+                nc.vector.tensor_copy(
+                    out=grp_t[u][:, c0 * PACK : (c0 + n) * PACK].bitcast(F32), in_=il[:, 0 : n * PACK].bitcast(F32)
+                )
 
         def quant(u):
             w = width(u)

@@ -22,10 +22,12 @@ NT = 512
 CHUNKS = ((0, 0, 1024), (1, 0, 1024), (2, 0, 1024), (0, 1024, 1024), (1, 1024, 1024), (2, 1024, 512), (2, 1536, 512))
 UNITS = len(CHUNKS) * PASSES
 V_PLANES = (3, 0, 2, 0, 0, 0, 0, 0, 0, 0, 0, 0, 0, 0, 0, 0, 0, 0, 1, 0, 0, 0, 1, 0, 0, 0, 0, 0)
-S_COLS = (0, 0, 0, 0, 0, 0, 0, 0, 0, 0, 0, 0, 0, 0, 0, 0, 0, 512, 256, 256, 0, 512, 0, 128, 0, 0, 256, 0)
-G_ADDS = 4
+S_COLS = (0, 0, 0, 0, 0, 0, 0, 0, 0, 0, 0, 0, 0, 0, 0, 0, 0, 512, 256, 256, 0, 512, 0, 0, 0, 0, 0, 0)
+GA = (4, 4, 4, 4)
 PE_MAX = 1024
 BURST = True
+SP = (26,)
+Q_FIRST = False
 X_AFTER = 1
 RUN = 8
 TABLE_STEP = 4
@@ -127,7 +129,8 @@ def tile_attention_pa_kernel(tc, x, rope, qkv_w_bytes, qkv_w_scale, out_0, out_1
             w = width(u)
             grp = grpp.tile([P, w * PACK], BF16, align_bytes=64)
             grp_t[u] = grp
-            cut = w - S_COLS[u]
+            sp = 256 if u in SP else 0
+            cut = w - S_COLS[u] - sp
             cv = cut - pe_cols(u)
             if cv > 0:
                 nc.vector.tensor_copy(
@@ -147,11 +150,22 @@ def tile_attention_pa_kernel(tc, x, rope, qkv_w_bytes, qkv_w_scale, out_0, out_1
                         start=True,
                         stop=True,
                     )
-            if cut < w:
+            if S_COLS[u]:
                 nc.scalar.copy(
-                    out=grp[:, cut * PACK : w * PACK].rearrange("p (c i t) -> p c t i", i=RUN, t=PACK),
-                    in_=wide_t[u][:, :, cut:w].rearrange("p t (c i) -> p c t i", i=RUN),
+                    out=grp[:, cut * PACK : (w - sp) * PACK].rearrange("p (c i t) -> p c t i", i=RUN, t=PACK),
+                    in_=wide_t[u][:, :, cut : w - sp].rearrange("p t (c i) -> p c t i", i=RUN),
                 )
+            for c0 in range(w - sp, w, 2 * P):
+                il = psum.tile([P, 2 * P * PACK], BF16, tag="bank")
+                for h in range(0, 2 * P, P):
+                    nc.tensor.matmul(
+                        out=il[:, h * PACK : (h + P) * PACK],
+                        lhsT=identb[:],
+                        rhs=wide_t[u][:, :, c0 + h : c0 + h + P].rearrange("p t c -> p c t"),
+                        start=True,
+                        stop=True,
+                    )
+                nc.scalar.copy(out=grp[:, c0 * PACK : (c0 + 2 * P) * PACK].bitcast(F32), in_=il[:].bitcast(F32))
 
         def evac(u):
             for c0, n, il in il_t[u]:
@@ -251,6 +265,8 @@ def tile_attention_pa_kernel(tc, x, rope, qkv_w_bytes, qkv_w_scale, out_0, out_1
         for s in range(UNITS + 3):
             if s < UNITS:
                 widen(s)
+            if Q_FIRST and s == UNITS:
+                quant(s - 2)
             if 1 <= s <= UNITS:
                 inter(s - 1)
             if s == 1:
@@ -268,7 +284,7 @@ def tile_attention_pa_kernel(tc, x, rope, qkv_w_bytes, qkv_w_scale, out_0, out_1
                     plain_out(job, True)
                 else:
                     ra, rb = rope_mults(job)
-                    if BURST and i < G_ADDS:
+                    if BURST and i >= 4 - GA[(0, 1, 3, 4).index(job[0])]:
                         rope_add(job, ra, rb, nc.gpsimd)
                     else:
                         late.append((job, ra, rb))
@@ -276,7 +292,7 @@ def tile_attention_pa_kernel(tc, x, rope, qkv_w_bytes, qkv_w_scale, out_0, out_1
                 evac(s - 1)
             if s == 2:
                 x_quant()
-            if 2 <= s <= UNITS + 1:
+            if 2 <= s <= UNITS + 1 and not (Q_FIRST and s == UNITS):
                 quant(s - 2)
             for job, ra, rb in late:
                 rope_add(job, ra, rb, nc.vector)

@@ -42,7 +42,7 @@ def tile_attention_pa_kernel(tc, x, rope, qkv_w_bytes, qkv_w_scale, out_0, out_1
         const = ctx.enter_context(tc.tile_pool(name="const", bufs=1))
         wpool = ctx.enter_context(tc.tile_pool(name="wpool", bufs=1))
         widep = ctx.enter_context(tc.tile_pool(name="widep", bufs=4))
-        grpp = ctx.enter_context(tc.tile_pool(name="grpp", bufs=2))
+        grpp = ctx.enter_context(tc.tile_pool(name="grpp", bufs=4))
         codep = ctx.enter_context(tc.tile_pool(name="codep", bufs=3))
         ropep = ctx.enter_context(tc.tile_pool(name="ropep", bufs=4))
         outp = ctx.enter_context(tc.tile_pool(name="outp", bufs=4))

@@ -20,14 +20,15 @@ PACK = 4
 PASSES = HID // (P * PACK)
 NT = 512
 CHUNKS = ((0, 0, 1024), (1, 0, 1024), (2, 0, 1024), (0, 1024, 1024), (1, 1024, 1024), (2, 1024, 512), (2, 1536, 512))
-UNITS = len(CHUNKS) * PASSES
-V_PLANES = (3, 0, 2, 0, 0, 0, 0, 0, 0, 0, 0, 0, 0, 0, 0, 0, 0, 0, 1, 0, 0, 0, 1, 0, 0, 0, 0, 0)
-S_COLS = (0, 0, 0, 0, 0, 0, 0, 0, 0, 0, 0, 0, 0, 0, 0, 0, 0, 512, 256, 256, 0, 512, 0, 0, 0, 0, 0, 0)
+UNIT_LIST = [(c, g, 0, CHUNKS[c][2]) for c in range(len(CHUNKS)) for g in range(PASSES)]
+UNITS = len(UNIT_LIST)
+OUT_W = 256
+V_PLANES = (3, 1, 1, 0, 1, 0, 0, 0, 1, 0, 0, 0, 1, 0, 0, 0, 1, 0, 0, 0, 0, 0, 0, 0, 0, 0, 0, 0)
+S_COLS = (0, 0, 0, 0, 0, 0, 0, 0, 0, 0, 0, 0, 0, 0, 0, 0, 0, 512, 0, 0, 0, 512, 0, 0, 0, 0, 0, 0)
 GA = (4, 4, 4, 4)
 PE_MAX = 1024
 BURST = True
-SP = (26,)
-Q_FIRST = False
+SP = {23: 1, 26: 1}
 X_AFTER = 1
 RUN = 8
 TABLE_STEP = 4
@@ -63,9 +64,8 @@ def tile_attention_pa_kernel(tc, x, rope, qkv_w_bytes, qkv_w_scale, out_0, out_1
         planes = {}
 
         def load_unit(u):
-            comp, col, w = CHUNKS[u // PASSES]
-            g = u % PASSES
-            c0 = comp * H * D + col
+            c, g, off, w = UNIT_LIST[u]
+            c0 = CHUNKS[c][0] * H * D + CHUNKS[c][1] + off
             if u == 0:
                 for t in range(PACK):
                     wb1 = wpool.tile([P, w], U8, name="wbytes0_%d" % t)
@@ -111,10 +111,10 @@ def tile_attention_pa_kernel(tc, x, rope, qkv_w_bytes, qkv_w_scale, out_0, out_1
             return 0
 
         def width(u):
-            return CHUNKS[u // PASSES][2]
+            return UNIT_LIST[u][3]
 
         def widen(u):
-            g = u % PASSES
+            g = UNIT_LIST[u][1]
             wide = widep.tile([P, PACK, width(u)], BF16)
             wide_t[u] = wide
             for t in range(PACK):
@@ -129,7 +129,7 @@ def tile_attention_pa_kernel(tc, x, rope, qkv_w_bytes, qkv_w_scale, out_0, out_1
             w = width(u)
             grp = grpp.tile([P, w * PACK], BF16, align_bytes=64)
             grp_t[u] = grp
-            sp = 256 if u in SP else 0
+            sp = 256 * SP.get(u, 0)
             cut = w - S_COLS[u] - sp
             cv = cut - pe_cols(u)
             if cv > 0:
@@ -204,30 +204,32 @@ def tile_attention_pa_kernel(tc, x, rope, qkv_w_bytes, qkv_w_scale, out_0, out_1
             nc.vector.quantize_mx(out=x_codes[:].bitcast(FP8X4), scales=x_scl[:], in_=x_grp[:])
 
         def mm(u):
-            c, g = u // PASSES, u % PASSES
+            c, g, off, w = UNIT_LIST[u]
             for b in range(B):
-                for nh in range(width(u) // NT):
+                for n0 in range(0, w, NT):
+                    n = min(NT, w)
+                    nh, o = divmod(off + n0, NT)
                     if g == 0:
                         acc = psum.tile([P, NT], F32, tag="bank")
                         acc_t[(c, b, nh)] = acc
                     xc = slice((g * B + b) * N, (g * B + b + 1) * N)
-                    wc = slice(nh * NT, (nh + 1) * NT)
+                    wc = slice(n0, n0 + n)
                     nc.tensor.matmul_mx(
-                        out=acc_t[(c, b, nh)][:],
+                        out=acc_t[(c, b, nh)][:, o : o + n],
                         lhsT=x_codes[:, xc].bitcast(FP8X4),
                         lhsT_scale=x_scl[:, xc],
                         rhs=code_t[u][:, wc].bitcast(FP8X4),
                         rhs_scale=scl_t[u][:, wc],
                         start=(g == 0),
-                        stop=(g == PASSES - 1),
+                        stop=(g == PASSES - 1 and o + n == NT),
                     )
 
-        def store(job, res):
+        def store(job, res, o=0, w=NT):
             c, b, nh = job
-            comp, col, w = CHUNKS[c]
-            h0 = (col + nh * NT) // D
+            comp, col, cw = CHUNKS[c]
+            h0 = (col + nh * NT + o) // D
             nc.sync.dma_start(
-                out=outs[comp][b, h0 : h0 + NT // D].rearrange("h n d -> n h d"),
+                out=outs[comp][b, h0 : h0 + w // D].rearrange("h n d -> n h d"),
                 in_=res[:].rearrange("p (h d) -> p h d", d=D),
             )
 
@@ -252,21 +254,20 @@ def tile_attention_pa_kernel(tc, x, rope, qkv_w_bytes, qkv_w_scale, out_0, out_1
             )
             store(job, res)
 
-        def plain_out(job, on_scalar):
-            res = outp.tile([P, NT], F32)
-            if on_scalar:
-                nc.scalar.copy(out=res[:], in_=acc_t[job][:])
-            else:
-                nc.vector.tensor_copy(out=res[:], in_=acc_t[job][:])
-            store(job, res)
+        def plain_out(job, on_scalar, w=NT):
+            for o in range(0, NT, w):
+                res = outp.tile([P, w], F32, tag="v%d" % w)
+                if on_scalar:
+                    nc.scalar.copy(out=res[:], in_=acc_t[job][:, o : o + w])
+                else:
+                    nc.vector.tensor_copy(out=res[:], in_=acc_t[job][:, o : o + w])
+                store(job, res, o, w)
 
         jobs = []
         done = 0
         for s in range(UNITS + 3):
             if s < UNITS:
                 widen(s)
-            if Q_FIRST and s == UNITS:
-                quant(s - 2)
             if 1 <= s <= UNITS:
                 inter(s - 1)
             if s == 1:
@@ -292,14 +293,14 @@ def tile_attention_pa_kernel(tc, x, rope, qkv_w_bytes, qkv_w_scale, out_0, out_1
                 evac(s - 1)
             if s == 2:
                 x_quant()
-            if 2 <= s <= UNITS + 1 and not (Q_FIRST and s == UNITS):
+            if 2 <= s <= UNITS + 1:
                 quant(s - 2)
             for job, ra, rb in late:
                 rope_add(job, ra, rb, nc.vector)
             if s >= 3:
                 mm(s - 3)
-                if (s - 3) % PASSES == PASSES - 1:
-                    c = (s - 3) // PASSES
+                c, g, off, w = UNIT_LIST[s - 3]
+                if g == PASSES - 1 and off + w == CHUNKS[c][2]:
                     jobs.extend([(c, b, nh) for b in range(B) for nh in range(CHUNKS[c][2] // NT)])
         for i, job in enumerate(jobs[done:]):
-            plain_out(job, i % 2 == 0)
+            plain_out(job, i % 2 == 0, OUT_W)

@@ -23,15 +23,17 @@ CHUNKS = ((0, 0, 1024), (1, 0, 1024), (2, 0, 1024), (0, 1024, 1024), (1, 1024, 1
 UNIT_LIST = [(c, g, 0, CHUNKS[c][2]) for c in range(len(CHUNKS)) for g in range(PASSES)]
 UNITS = len(UNIT_LIST)
 OUT_W = 256
-V_PLANES = (3, 1, 1, 0, 1, 0, 0, 0, 1, 0, 0, 0, 1, 0, 0, 0, 1, 0, 0, 0, 0, 0, 0, 0, 0, 0, 0, 0)
-S_COLS = (0, 0, 0, 0, 0, 0, 0, 0, 0, 0, 0, 0, 0, 0, 0, 0, 0, 512, 0, 0, 0, 512, 0, 0, 0, 0, 0, 0)
+V_PLANES = (3, 1, 1, 1, 0, 0, 1, 0, 0, 1, 0, 0, 1, 0, 0, 0, 0, 0, 0, 0, 0, 0, 0, 0, 0, 0, 0, 0)
+S_COLS = (0, 0, 0, 0, 0, 0, 0, 0, 0, 0, 0, 0, 0, 0, 0, 0, 0, 0, 0, 0, 0, 512, 0, 0, 0, 0, 0, 0)
 GA = (4, 4, 4, 4)
-PE_MAX = 1024
+COVER = 4
+EXT = {23: 2}
+BANK = 256
 BURST = True
-SP = {23: 1, 26: 1}
+SP = {17: 2, 26: 1}
 X_AFTER = 1
 RUN = 8
-TABLE_STEP = 4
+TABLE_STEP = 1
 
 
 def tile_attention_pa_kernel(tc, x, rope, qkv_w_bytes, qkv_w_scale, out_0, out_1, out_2):
@@ -96,18 +98,18 @@ def tile_attention_pa_kernel(tc, x, rope, qkv_w_bytes, qkv_w_scale, out_0, out_1
         def rope_table():
             rv = rope_sb[:].rearrange("p (j e) -> p j e", e=2)
             sv = tab[:, 1, :].rearrange("p (j e) -> p j e", e=2)
-            nc.vector.tensor_copy(
+            nc.gpsimd.tensor_copy(
                 out=tab[:, 0, :].rearrange("p (j e) -> p j e", e=2), in_=rv[:, :, 0:1].to_broadcast([P, D // 2, 2])
             )
-            nc.vector.tensor_copy(out=sv[:, :, 0:1], in_=rv[:, :, 1:2])
-            nc.vector.tensor_scalar(out=sv[:, :, 1:2], in0=rv[:, :, 1:2], scalar1=-1.0, scalar2=None, op0=ALU.mult)
+            nc.gpsimd.tensor_copy(out=sv[:, :, 0:1], in_=rv[:, :, 1:2])
+            nc.gpsimd.tensor_scalar(out=sv[:, :, 1:2], in0=rv[:, :, 1:2], scalar1=-1.0, scalar2=None, op0=ALU.mult)
 
         wide_t, grp_t, code_t, scl_t, acc_t, il_t = {}, {}, {}, {}, {}, {}
 
         def pe_cols(u):
             c = u - PASSES - 2
             if c >= 0 and c % PASSES == 0 and CHUNKS[c // PASSES][0] != 2:
-                return min(PE_MAX, width(u) - S_COLS[u])
+                return min(BANK * COVER, width(u) - S_COLS[u] - BANK * SP.get(u, 0))
             return 0
 
         def width(u):
@@ -125,53 +127,44 @@ def tile_attention_pa_kernel(tc, x, rope, qkv_w_bytes, qkv_w_scale, out_0, out_1
                 else:
                     nc.scalar.activation(out=wide[:, t, :], in_=src, func=ACT.Copy, scale=col)
 
+        def turn(u, c0):
+            il = psum.tile([P, BANK * PACK], BF16, tag="bank")
+            for h in range(0, BANK, P):
+                nc.tensor.matmul(
+                    out=il[:, h * PACK : (h + P) * PACK],
+                    lhsT=identb[:],
+                    rhs=wide_t[u][:, :, c0 + h : c0 + h + P].rearrange("p t c -> p c t"),
+                    start=True,
+                    stop=True,
+                )
+            return il
+
         def inter(u):
             w = width(u)
             grp = grpp.tile([P, w * PACK], BF16, align_bytes=64)
             grp_t[u] = grp
-            sp = 256 * SP.get(u, 0)
+            sp = BANK * SP.get(u, 0)
             cut = w - S_COLS[u] - sp
-            cv = cut - pe_cols(u)
+            cv = cut - max(pe_cols(u), BANK * EXT.get(u, 0))
             if cv > 0:
                 nc.vector.tensor_copy(
                     out=grp[:, 0 : cv * PACK].rearrange("p (c i t) -> p c t i", i=RUN, t=PACK),
                     in_=wide_t[u][:, :, 0:cv].rearrange("p t (c i) -> p c t i", i=RUN),
                 )
-            il_t[u] = []
-            for c0 in range(cv, cut, 2 * P):
-                n = min(2 * P, cut - c0)
-                il = psum.tile([P, 2 * P * PACK], BF16, tag="bank")
-                il_t[u].append((c0, n, il))
-                for h in range(0, n, P):
-                    nc.tensor.matmul(
-                        out=il[:, h * PACK : (h + P) * PACK],
-                        lhsT=identb[:],
-                        rhs=wide_t[u][:, :, c0 + h : c0 + h + P].rearrange("p t c -> p c t"),
-                        start=True,
-                        stop=True,
-                    )
+            il_t[u] = range(cv, cut, BANK)
             if S_COLS[u]:
                 nc.scalar.copy(
                     out=grp[:, cut * PACK : (w - sp) * PACK].rearrange("p (c i t) -> p c t i", i=RUN, t=PACK),
                     in_=wide_t[u][:, :, cut : w - sp].rearrange("p t (c i) -> p c t i", i=RUN),
                 )
-            for c0 in range(w - sp, w, 2 * P):
-                il = psum.tile([P, 2 * P * PACK], BF16, tag="bank")
-                for h in range(0, 2 * P, P):
-                    nc.tensor.matmul(
-                        out=il[:, h * PACK : (h + P) * PACK],
-                        lhsT=identb[:],
-                        rhs=wide_t[u][:, :, c0 + h : c0 + h + P].rearrange("p t c -> p c t"),
-                        start=True,
-                        stop=True,
-                    )
-                nc.scalar.copy(out=grp[:, c0 * PACK : (c0 + 2 * P) * PACK].bitcast(F32), in_=il[:].bitcast(F32))
+            for c0 in range(w - sp, w, BANK):
+                il = turn(u, c0)
+                nc.scalar.copy(out=grp[:, c0 * PACK : (c0 + BANK) * PACK].bitcast(F32), in_=il[:].bitcast(F32))
 
         def evac(u):
-            for c0, n, il in il_t[u]:
-                nc.vector.tensor_copy(
-                    out=grp_t[u][:, c0 * PACK : (c0 + n) * PACK].bitcast(F32), in_=il[:, 0 : n * PACK].bitcast(F32)
-                )
+            turned = [(c0, turn(u, c0)) for c0 in il_t[u]]
+            for c0, il in turned:
+                nc.vector.tensor_copy(out=grp_t[u][:, c0 * PACK : (c0 + BANK) * PACK].bitcast(F32), in_=il[:].bitcast(F32))
 
         def quant(u):
             w = width(u)
@@ -268,8 +261,10 @@ def tile_attention_pa_kernel(tc, x, rope, qkv_w_bytes, qkv_w_scale, out_0, out_1
         for s in range(UNITS + 3):
             if s < UNITS:
                 widen(s)
-            if 1 <= s <= UNITS:
+            if 1 <= s <= UNITS and s - 1 not in EXT:
                 inter(s - 1)
+            if s in EXT:
+                inter(s)
             if s == 1:
                 x_transposes()
             if s == TABLE_STEP:
@@ -289,8 +284,10 @@ def tile_attention_pa_kernel(tc, x, rope, qkv_w_bytes, qkv_w_scale, out_0, out_1
                         rope_add(job, ra, rb, nc.gpsimd)
                     else:
                         late.append((job, ra, rb))
-            if 1 <= s <= UNITS:
+            if 1 <= s <= UNITS and s - 1 not in EXT:
                 evac(s - 1)
+            if s in EXT:
+                evac(s)
             if s == 2:
                 x_quant()
             if 2 <= s <= UNITS + 1:

@@ -23,15 +23,16 @@ CHUNKS = ((0, 0, 1024), (1, 0, 1024), (2, 0, 1024), (0, 1024, 1024), (1, 1024, 1
 UNIT_LIST = [(c, g, 0, CHUNKS[c][2]) for c in range(len(CHUNKS)) for g in range(PASSES)]
 UNITS = len(UNIT_LIST)
 OUT_W = 256
-V_PLANES = (3, 1, 1, 1, 0, 0, 1, 0, 0, 1, 0, 0, 1, 0, 0, 0, 0, 0, 0, 0, 0, 0, 0, 0, 0, 0, 0, 0)
+V_PLANES = (3, 0, 1, 1, 0, 1, 0, 0, 0, 1, 0, 0, 0, 1, 0, 0, 0, 1, 0, 0, 0, 0, 0, 0, 0, 0, 0, 0)
 S_COLS = (0, 0, 0, 0, 0, 0, 0, 0, 0, 0, 0, 0, 0, 0, 0, 0, 0, 0, 0, 0, 0, 512, 0, 0, 0, 0, 0, 0)
-GA = (4, 4, 4, 4)
+FIRST_JOB = (512,)
+RR_BUFS = 4
 COVER = 4
 EXT = {23: 2}
 BANK = 256
-BURST = True
 SP = {17: 2, 26: 1}
 X_AFTER = 1
+SPLIT = 2
 RUN = 8
 TABLE_STEP = 1
 
@@ -47,7 +48,7 @@ def tile_attention_pa_kernel(tc, x, rope, qkv_w_bytes, qkv_w_scale, out_0, out_1
         widep = ctx.enter_context(tc.tile_pool(name="widep", bufs=4))
         grpp = ctx.enter_context(tc.tile_pool(name="grpp", bufs=4))
         codep = ctx.enter_context(tc.tile_pool(name="codep", bufs=3))
-        ropep = ctx.enter_context(tc.tile_pool(name="ropep", bufs=4))
+        ropep = ctx.enter_context(tc.tile_pool(name="ropep", bufs=RR_BUFS))
         outp = ctx.enter_context(tc.tile_pool(name="outp", bufs=4))
         psum = ctx.enter_context(tc.psum_pool(name="psum", bufs=8))
 
@@ -68,9 +69,9 @@ def tile_attention_pa_kernel(tc, x, rope, qkv_w_bytes, qkv_w_scale, out_0, out_1
         def load_unit(u):
             c, g, off, w = UNIT_LIST[u]
             c0 = CHUNKS[c][0] * H * D + CHUNKS[c][1] + off
-            if u == 0:
+            if u < SPLIT:
                 for t in range(PACK):
-                    wb1 = wpool.tile([P, w], U8, name="wbytes0_%d" % t)
+                    wb1 = wpool.tile([P, w], U8, name="wbytes%d_%d" % (u, t))
                     nc.sync.dma_start(out=wb1[:], in_=wb_view[g, :, t, c0 : c0 + w])
                     planes[(u, t)] = wb1[:]
             else:
@@ -226,25 +227,25 @@ def tile_attention_pa_kernel(tc, x, rope, qkv_w_bytes, qkv_w_scale, out_0, out_1
                 in_=res[:].rearrange("p (h d) -> p h d", d=D),
             )
 
-        def rope_mults(job):
+        def rope(job, widths):
             acc = acc_t[job]
-            rr = ropep.tile([P, 2, NT], F32)
-            nc.vector.tensor_tensor(
-                out=rr[:].rearrange("p r (h d) -> p r h d", d=D),
-                in0=acc[:].rearrange("p (o h d) -> p o h d", o=1, d=D).to_broadcast([P, 2, NT // D, D]),
-                in1=tab[:].rearrange("p r (o d) -> p r o d", o=1).to_broadcast([P, 2, NT // D, D]),
-                op=ALU.mult,
-            )
-            return rr[:, 0, :], rr[:, 1, :]
-
-        def rope_add(job, ra, rb, engine):
             res = outp.tile([P, NT], F32)
-            engine.tensor_tensor(
-                out=res[:].rearrange("p (j e) -> p j e", e=2),
-                in0=ra.rearrange("p (j e) -> p j e", e=2),
-                in1=rb.rearrange("p (j e) -> p j e", e=2)[:, :, ::-1],
-                op=ALU.add,
-            )
+            o = 0
+            for w in widths:
+                rr = ropep.tile([P, 2, w], F32, tag="rr")
+                nc.vector.tensor_tensor(
+                    out=rr[:].rearrange("p r (h d) -> p r h d", d=D),
+                    in0=acc[:, o : o + w].rearrange("p (o h d) -> p o h d", o=1, d=D).to_broadcast([P, 2, w // D, D]),
+                    in1=tab[:].rearrange("p r (o d) -> p r o d", o=1).to_broadcast([P, 2, w // D, D]),
+                    op=ALU.mult,
+                )
+                nc.gpsimd.tensor_tensor(
+                    out=res[:, o : o + w].rearrange("p (j e) -> p j e", e=2),
+                    in0=rr[:, 0, :].rearrange("p (j e) -> p j e", e=2),
+                    in1=rr[:, 1, :].rearrange("p (j e) -> p j e", e=2)[:, :, ::-1],
+                    op=ALU.add,
+                )
+                o += w
             store(job, res)
 
         def plain_out(job, on_scalar, w=NT):
@@ -269,21 +270,14 @@ def tile_attention_pa_kernel(tc, x, rope, qkv_w_bytes, qkv_w_scale, out_0, out_1
                 x_transposes()
             if s == TABLE_STEP:
                 rope_table()
-            late = []
             take = len(jobs) - done
-            if not BURST:
-                take = min(1, take)
             for i in range(take):
                 job = jobs[done]
                 done += 1
                 if CHUNKS[job[0]][0] == 2:
                     plain_out(job, True)
                 else:
-                    ra, rb = rope_mults(job)
-                    if BURST and i >= 4 - GA[(0, 1, 3, 4).index(job[0])]:
-                        rope_add(job, ra, rb, nc.gpsimd)
-                    else:
-                        late.append((job, ra, rb))
+                    rope(job, FIRST_JOB if i == 0 else (NT,))
             if 1 <= s <= UNITS and s - 1 not in EXT:
                 evac(s - 1)
             if s in EXT:
@@ -292,8 +286,6 @@ def tile_attention_pa_kernel(tc, x, rope, qkv_w_bytes, qkv_w_scale, out_0, out_1
                 x_quant()
             if 2 <= s <= UNITS + 1:
                 quant(s - 2)
-            for job, ra, rb in late:
-                rope_add(job, ra, rb, nc.vector)
             if s >= 3:
                 mm(s - 3)
                 c, g, off, w = UNIT_LIST[s - 3]

from contextlib import ExitStack

import concourse.mybir as mybir
from concourse.masks import make_identity

F32 = mybir.dt.float32
BF16 = mybir.dt.bfloat16
U32 = mybir.dt.uint32
U8 = mybir.dt.uint8
FP8 = mybir.dt.float8_e4m3fn
FP8X4 = mybir.dt.float8_e4m3fn_x4
ACT = mybir.ActivationFunctionType
ALU = mybir.AluOpType

B, N, HID, H, D = 2, 128, 2048, 16, 128
FLOPS = 2 * B * N * HID * 3 * H * D

P = 128
PACK = 4
PASSES = HID // (P * PACK)
NT = 512
CHUNKS = ((0, 0, 1024), (1, 0, 1024), (2, 0, 1024), (0, 1024, 1024), (1, 1024, 1024), (2, 1024, 512), (2, 1536, 512))
UNIT_LIST = [(c, g, 0, CHUNKS[c][2]) for c in range(len(CHUNKS)) for g in range(PASSES)]
UNITS = len(UNIT_LIST)
OUT_W = 256
V_PLANES = (3, 0, 1, 1, 0, 1, 0, 0, 0, 1, 0, 0, 0, 1, 0, 0, 0, 1, 0, 0, 0, 0, 0, 0, 0, 0, 0, 0)
S_COLS = (0, 0, 0, 0, 0, 0, 0, 0, 0, 0, 0, 0, 0, 0, 0, 0, 0, 0, 0, 0, 0, 512, 0, 0, 0, 0, 0, 0)
FIRST_JOB = (512,)
RR_BUFS = 4
COVER = 4
EXT = {23: 2}
BANK = 256
SP = {17: 2, 26: 1}
X_AFTER = 1
SPLIT = 2
RUN = 8
TABLE_STEP = 1


def tile_attention_pa_kernel(tc, x, rope, qkv_w_bytes, qkv_w_scale, out_0, out_1, out_2):
    nc = tc.nc
    outs = (out_0, out_1, out_2)
    wb_view = qkv_w_bytes.rearrange("(g p t) n -> g p t n", p=P, t=PACK)

    with ExitStack() as ctx:
        const = ctx.enter_context(tc.tile_pool(name="const", bufs=1))
        wpool = ctx.enter_context(tc.tile_pool(name="wpool", bufs=1))
        widep = ctx.enter_context(tc.tile_pool(name="widep", bufs=4))
        grpp = ctx.enter_context(tc.tile_pool(name="grpp", bufs=4))
        codep = ctx.enter_context(tc.tile_pool(name="codep", bufs=3))
        ropep = ctx.enter_context(tc.tile_pool(name="ropep", bufs=RR_BUFS))
        outp = ctx.enter_context(tc.tile_pool(name="outp", bufs=4))
        psum = ctx.enter_context(tc.psum_pool(name="psum", bufs=8))

        ident = const.tile([P, P], F32)
        make_identity(nc, ident[:])
        identb = const.tile([P, P], BF16)
        make_identity(nc, identb[:])

        ctx.enter_context(tc.manual_schedule())

        wscale = const.tile([P, PASSES * PACK], F32)
        nc.scalar.dma_start(
            out=wscale[:].rearrange("p (g t) -> p g t", t=PACK),
            in_=qkv_w_scale.rearrange("(g p t) o -> p g (t o)", p=P, t=PACK),
        )
        planes = {}

        def load_unit(u):
            c, g, off, w = UNIT_LIST[u]
            c0 = CHUNKS[c][0] * H * D + CHUNKS[c][1] + off
            if u < SPLIT:
                for t in range(PACK):
                    wb1 = wpool.tile([P, w], U8, name="wbytes%d_%d" % (u, t))
                    nc.sync.dma_start(out=wb1[:], in_=wb_view[g, :, t, c0 : c0 + w])
                    planes[(u, t)] = wb1[:]
            else:
                wb = wpool.tile([P, PACK, w], U8, name="wbytes%d" % u)
                nc.sync.dma_start(out=wb[:], in_=wb_view[g, :, :, c0 : c0 + w])
                for t in range(PACK):
                    planes[(u, t)] = wb[:, t, :]

        x_sb = const.tile([P, B, HID], BF16)
        rope_sb = const.tile([P, D], BF16)
        for u in range(UNITS):
            load_unit(u)
            if u == X_AFTER:
                for b in range(B):
                    nc.sync.dma_start(out=x_sb[:, b, :], in_=x[b])
                nc.sync.dma_start(out=rope_sb[:], in_=rope.rearrange("n o d -> n (o d)"))

        warm = const.tile([P, 1], F32)
        warm2 = const.tile([P, 1], F32)
        nc.gpsimd.memset(warm[:], 0.0)
        nc.scalar.activation(out=warm2[:], in_=warm[:], func=ACT.Copy)

        tab = const.tile([P, 2, D], F32)

        def rope_table():
            rv = rope_sb[:].rearrange("p (j e) -> p j e", e=2)
            sv = tab[:, 1, :].rearrange("p (j e) -> p j e", e=2)
            nc.gpsimd.tensor_copy(
                out=tab[:, 0, :].rearrange("p (j e) -> p j e", e=2), in_=rv[:, :, 0:1].to_broadcast([P, D // 2, 2])
            )
            nc.gpsimd.tensor_copy(out=sv[:, :, 0:1], in_=rv[:, :, 1:2])
            nc.gpsimd.tensor_scalar(out=sv[:, :, 1:2], in0=rv[:, :, 1:2], scalar1=-1.0, scalar2=None, op0=ALU.mult)

        wide_t, grp_t, code_t, scl_t, acc_t, il_t = {}, {}, {}, {}, {}, {}

        def pe_cols(u):
            c = u - PASSES - 2
            if c >= 0 and c % PASSES == 0 and CHUNKS[c // PASSES][0] != 2:
                return min(BANK * COVER, width(u) - S_COLS[u] - BANK * SP.get(u, 0))
            return 0

        def width(u):
            return UNIT_LIST[u][3]

        def widen(u):
            g = UNIT_LIST[u][1]
            wide = widep.tile([P, PACK, width(u)], BF16)
            wide_t[u] = wide
            for t in range(PACK):
                col = wscale[:, PACK * g + t : PACK * g + t + 1]
                src = planes[(u, t)].bitcast(FP8)
                if t >= PACK - V_PLANES[u]:
                    nc.vector.tensor_scalar(out=wide[:, t, :], in0=src, scalar1=col, scalar2=None, op0=ALU.mult)
                else:
                    nc.scalar.activation(out=wide[:, t, :], in_=src, func=ACT.Copy, scale=col)

        def turn(u, c0):
            il = psum.tile([P, BANK * PACK], BF16, tag="bank")
            for h in range(0, BANK, P):
                nc.tensor.matmul(
                    out=il[:, h * PACK : (h + P) * PACK],
                    lhsT=identb[:],
                    rhs=wide_t[u][:, :, c0 + h : c0 + h + P].rearrange("p t c -> p c t"),
                    start=True,
                    stop=True,
                )
            return il

        def inter(u):
            w = width(u)
            grp = grpp.tile([P, w * PACK], BF16, align_bytes=64)
            grp_t[u] = grp
            sp = BANK * SP.get(u, 0)
            cut = w - S_COLS[u] - sp
            cv = cut - max(pe_cols(u), BANK * EXT.get(u, 0))
            if cv > 0:
                nc.vector.tensor_copy(
                    out=grp[:, 0 : cv * PACK].rearrange("p (c i t) -> p c t i", i=RUN, t=PACK),
                    in_=wide_t[u][:, :, 0:cv].rearrange("p t (c i) -> p c t i", i=RUN),
                )
            il_t[u] = range(cv, cut, BANK)
            if S_COLS[u]:
                nc.scalar.copy(
                    out=grp[:, cut * PACK : (w - sp) * PACK].rearrange("p (c i t) -> p c t i", i=RUN, t=PACK),
                    in_=wide_t[u][:, :, cut : w - sp].rearrange("p t (c i) -> p c t i", i=RUN),
                )
            for c0 in range(w - sp, w, BANK):
                il = turn(u, c0)
                nc.scalar.copy(out=grp[:, c0 * PACK : (c0 + BANK) * PACK].bitcast(F32), in_=il[:].bitcast(F32))

        def evac(u):
            turned = [(c0, turn(u, c0)) for c0 in il_t[u]]
            for c0, il in turned:
                nc.vector.tensor_copy(out=grp_t[u][:, c0 * PACK : (c0 + BANK) * PACK].bitcast(F32), in_=il[:].bitcast(F32))

        def quant(u):
            w = width(u)
            codes = codep.tile([P, w], U32, align_bytes=64)
            scl = codep.tile([P, w], U8, align_bytes=64)
            code_t[u] = codes
            scl_t[u] = scl
            nc.vector.quantize_mx(out=codes[:].bitcast(FP8X4), scales=scl[:], in_=grp_t[u][:])

        x_grp = const.tile([P, PASSES * B * N * PACK], BF16, align_bytes=64)
        x_codes = const.tile([P, PASSES * B * N], U32, align_bytes=64)
        x_scl = const.tile([P, PASSES * B * N], U8, align_bytes=64)

        def x_transposes():
            xw = x_grp[:].bitcast(F32).rearrange("p (g b r u) -> p g b r u", g=PASSES, b=B, u=2)
            for b in range(B):
                words = x_sb[:, b, :].bitcast(F32)
                for gp in range(PASSES // 2):
                    xt = psum.tile([P, 4, N], F32, tag="bank")
                    for gl in range(2):
                        g = 2 * gp + gl
                        for u in range(2):
                            nc.tensor.transpose(xt[:, 2 * gl + u, :], words[:, 256 * g + u : 256 * (g + 1) : 2], ident[:])
                    nc.vector.tensor_copy(
                        out=xw[:, 2 * gp : 2 * gp + 2, b, :, :],
                        in_=xt[:].rearrange("p (g u) r -> p g r u", u=2),
                    )

        def x_quant():
            nc.vector.quantize_mx(out=x_codes[:].bitcast(FP8X4), scales=x_scl[:], in_=x_grp[:])

        def mm(u):
            c, g, off, w = UNIT_LIST[u]
            for b in range(B):
                for n0 in range(0, w, NT):
                    n = min(NT, w)
                    nh, o = divmod(off + n0, NT)
                    if g == 0:
                        acc = psum.tile([P, NT], F32, tag="bank")
                        acc_t[(c, b, nh)] = acc
                    xc = slice((g * B + b) * N, (g * B + b + 1) * N)
                    wc = slice(n0, n0 + n)
                    nc.tensor.matmul_mx(
                        out=acc_t[(c, b, nh)][:, o : o + n],
                        lhsT=x_codes[:, xc].bitcast(FP8X4),
                        lhsT_scale=x_scl[:, xc],
                        rhs=code_t[u][:, wc].bitcast(FP8X4),
                        rhs_scale=scl_t[u][:, wc],
                        start=(g == 0),
                        stop=(g == PASSES - 1 and o + n == NT),
                    )

        def store(job, res, o=0, w=NT):
            c, b, nh = job
            comp, col, cw = CHUNKS[c]
            h0 = (col + nh * NT + o) // D
            nc.sync.dma_start(
                out=outs[comp][b, h0 : h0 + w // D].rearrange("h n d -> n h d"),
                in_=res[:].rearrange("p (h d) -> p h d", d=D),
            )

        def rope(job, widths):
            acc = acc_t[job]
            res = outp.tile([P, NT], F32)
            o = 0
            for w in widths:
                rr = ropep.tile([P, 2, w], F32, tag="rr")
                nc.vector.tensor_tensor(
                    out=rr[:].rearrange("p r (h d) -> p r h d", d=D),
                    in0=acc[:, o : o + w].rearrange("p (o h d) -> p o h d", o=1, d=D).to_broadcast([P, 2, w // D, D]),
                    in1=tab[:].rearrange("p r (o d) -> p r o d", o=1).to_broadcast([P, 2, w // D, D]),
                    op=ALU.mult,
                )
                nc.gpsimd.tensor_tensor(
                    out=res[:, o : o + w].rearrange("p (j e) -> p j e", e=2),
                    in0=rr[:, 0, :].rearrange("p (j e) -> p j e", e=2),
                    in1=rr[:, 1, :].rearrange("p (j e) -> p j e", e=2)[:, :, ::-1],
                    op=ALU.add,
                )
                o += w
            store(job, res)

        def plain_out(job, on_scalar, w=NT):
            for o in range(0, NT, w):
                res = outp.tile([P, w], F32, tag="v%d" % w)
                if on_scalar:
                    nc.scalar.copy(out=res[:], in_=acc_t[job][:, o : o + w])
                else:
                    nc.vector.tensor_copy(out=res[:], in_=acc_t[job][:, o : o + w])
                store(job, res, o, w)

        jobs = []
        done = 0
        for s in range(UNITS + 3):
            if s < UNITS:
                widen(s)
            if 1 <= s <= UNITS and s - 1 not in EXT:
                inter(s - 1)
            if s in EXT:
                inter(s)
            if s == 1:
                x_transposes()
            if s == TABLE_STEP:
                rope_table()
            take = len(jobs) - done
            for i in range(take):
                job = jobs[done]
                done += 1
                if CHUNKS[job[0]][0] == 2:
                    plain_out(job, True)
                else:
                    rope(job, FIRST_JOB if i == 0 else (NT,))
            if 1 <= s <= UNITS and s - 1 not in EXT:
                evac(s - 1)
            if s in EXT:
                evac(s)
            if s == 2:
                x_quant()
            if 2 <= s <= UNITS + 1:
                quant(s - 2)
            if s >= 3:
                mm(s - 3)
                c, g, off, w = UNIT_LIST[s - 3]
                if g == PASSES - 1 and off + w == CHUNKS[c][2]:
                    jobs.extend([(c, b, nh) for b in range(B) for nh in range(CHUNKS[c][2] // NT)])
        for i, job in enumerate(jobs[done:]):
            plain_out(job, i % 2 == 0, OUT_W)
